import numpy as np
import ml_dtypes


def mxq(x, axis, fmt="e4m3"):
    dtype, down = {"e4m3": (ml_dtypes.float8_e4m3fn, 7), "e5m2": (ml_dtypes.float8_e5m2, 14)}[fmt]
    v = np.moveaxis(np.asarray(x, np.float32).astype(ml_dtypes.bfloat16).astype(np.float64), axis, -1)
    blocks = v.reshape(v.shape[:-1] + (-1, 32))
    amax = np.abs(blocks).max(-1, keepdims=True)
    byte = np.maximum(np.where(amax > 0, np.frexp(amax)[1] - 1 + 127, 0) - down, 1)
    scale = np.exp2(byte - 127.0)
    codes = (blocks / scale).astype(np.float32).astype(dtype).astype(np.float64)
    return np.moveaxis((codes * scale).reshape(v.shape), -1, axis)


WIDE = False


def mx_kscale(k):
    if not WIDE:
        return np.ones(k)
    levels = np.array([20, -20, 10, -10, 0])
    a = np.random.permutation(np.resize(levels, k // 512 * 4)).reshape(k // 512, 4)
    idx = np.arange(k)
    return np.exp2(a[idx // 512, idx % 128 // 32])


BF16 = ml_dtypes.bfloat16


def bf(x):
    return np.asarray(x, np.float32).astype(BF16)


def f64(x):
    return np.asarray(x).astype(np.float64)


BLOCK_M, BLOCK_N = 128, 128
B, S, I, O = 1, 512, 2048, 4608


def setup_inputs():
    u = mx_kscale(O)
    sm, sn = O // BLOCK_M, I // BLOCK_N
    inp = np.random.standard_normal((B, S, I))
    weight = np.random.standard_normal((O, I)) / u[:, None]
    wsi = np.random.uniform(0.25, 1.0, (sm, sn)) * 0.035
    g = np.random.standard_normal((B, S, O)) * np.exp2(np.random.randint(-12, 1, (B, S, 1))) * 16.0 * u
    return {"input": bf(inp), "weight": bf(weight), "weight_scale_inv": bf(wsi), "grad_out": bf(g)}


def dequant_block_fp8_weight(weight, weight_scale_inv):
    sm, sn = weight_scale_inv.shape
    w = weight.reshape(sm, BLOCK_M, sn, BLOCK_N)
    w = w * weight_scale_inv[:, None, :, None]
    return w.reshape(sm * BLOCK_M, sn * BLOCK_N)


def reference(input, weight, weight_scale_inv, grad_out):
    dq_w = dequant_block_fp8_weight(f64(weight), f64(weight_scale_inv))
    return mxq(f64(grad_out), 2, "e5m2") @ mxq(dq_w, 0, "e4m3")

@@ -1,0 +1,193 @@
+from contextlib import ExitStack
+
+import concourse.mybir as mybir
+from concourse.masks import make_identity
+
+F32 = mybir.dt.float32
+BF16 = mybir.dt.bfloat16
+I32 = mybir.dt.int32
+U32 = mybir.dt.uint32
+U8 = mybir.dt.uint8
+E4M3X4 = mybir.dt.float8_e4m3fn_x4
+E5M2X4 = mybir.dt.float8_e5m2_x4
+MULT = mybir.AluOpType.mult
+COPY = mybir.ActivationFunctionType.Copy
+
+P = 128
+PACK = 4
+K_PASS = P * PACK
+TOKENS = 512
+K_ALL = 4608
+I_ALL = 2048
+PASSES = K_ALL // K_PASS
+HALF = I_ALL // 2
+M_TILES = TOKENS // P
+CHUNKS = 2 * PASSES
+RAW_BUFS = 8
+N_VEC = [5, 4, 4]
+
+FLOPS = 2 * TOKENS * K_ALL * I_ALL
+BYTES = K_ALL * I_ALL * 2 + TOKENS * K_ALL * 2 + 36 * 16 * 2 + TOKENS * I_ALL * 4
+
+
+def tile_gaudifp8linear_kernel(tc, inp, weight, weight_scale_inv, grad_out, out):
+    nc = tc.nc
+    g_dram = grad_out.flatten_outer_dims()
+    o_dram = out.flatten_outer_dims()
+
+    with ExitStack() as ctx:
+        const = ctx.enter_context(tc.tile_pool(name="const", bufs=1))
+        ggp = ctx.enter_context(tc.tile_pool(name="ggp", bufs=2))
+        rawp = ctx.enter_context(tc.tile_pool(name="rawp", bufs=RAW_BUFS))
+        grpp = ctx.enter_context(tc.tile_pool(name="grpp", bufs=3))
+        codp = ctx.enter_context(tc.tile_pool(name="codp", bufs=4))
+        outp = ctx.enter_context(tc.tile_pool(name="outp", bufs=8))
+        psum = ctx.enter_context(tc.psum_pool(name="psum", bufs=1))
+        ctx.enter_context(tc.manual_schedule())
+
+        sel = const.tile([P, P], BF16, name="sel")
+        nc.vector.memset(sel[:].bitcast(I32), 0)
+        for q in range(4):
+            nc.vector.memset(sel[32 * q : 32 * q + 32, 32 * q : 32 * q + 32], 1.0)
+        rows = const.tile([P, 256], BF16, name="rows")
+        nc.vector.memset(rows[:].bitcast(I32), 0)
+        warm = const.tile([P, 2], BF16, name="warm")
+        nc.scalar.activation(out=warm[:], in_=sel[:, 0:2], func=COPY)
+        ident = const.tile([P, P], F32, name="ident")
+        make_identity(nc, ident[:])
+
+        nc.sync.dma_start(
+            out=rows[0:P:32, 0 : 16 * PASSES].rearrange("q (c n) -> q c n", n=16),
+            in_=weight_scale_inv.rearrange("(c q) n -> q c n", q=4),
+        )
+
+        def load_w(i):
+            h, c = divmod(i, PASSES)
+            raw = rawp.tile([P, PACK, HALF], BF16, name="raw")
+            nc.sync.dma_start(
+                out=raw[:],
+                in_=weight[K_PASS * c : K_PASS * (c + 1), HALF * h : HALF * (h + 1)].rearrange(
+                    "(p j) w -> p j w", j=PACK
+                ),
+            )
+            return raw
+
+        raws = {}
+        raws[0] = load_w(0)
+        g_sb = []
+        for m in range(M_TILES):
+            g_t = const.tile([P, K_ALL], BF16, name="g%d" % m)
+            nc.sync.dma_start(out=g_t[:], in_=g_dram[P * m : P * (m + 1), :])
+            g_sb.append(g_t)
+        for i in range(1, RAW_BUFS):
+            raws[i] = load_w(i)
+
+        scl_ps = psum.tile([P, 512], F32, tag="b7", name="scl_ps")
+        nc.tensor.matmul(scl_ps[:, 0:256], lhsT=sel[:], rhs=rows[:], start=True, stop=True)
+        scl = const.tile([P, 16 * PASSES], F32, name="scl")
+        nc.vector.tensor_copy(out=scl[:], in_=scl_ps[:, 0 : 16 * PASSES])
+
+        gc = const.tile([P, M_TILES * PASSES * P], U32, name="gc", align_bytes=64)
+        gs = const.tile([P, M_TILES * PASSES * P], U8, name="gs", align_bytes=64)
+
+        def regroup(i):
+            h, c = divmod(i, PASSES)
+            raw = raws[i]
+            n_vec = N_VEC[i % len(N_VEC)]
+            grp = grpp.tile([P, HALF, PACK], BF16, name="grp", align_bytes=64)
+            for b in range(8):
+                cols = slice(P * b, P * (b + 1))
+                dst = grp[:, cols, :].rearrange("p (a i) t -> p a t i", i=4)
+                src = raw[:, :, cols].rearrange("p t (a i) -> p a t i", i=4)
+                col = 16 * c + 8 * h + b
+                fac = scl[:, col : col + 1]
+                if b < n_vec:
+                    nc.vector.tensor_scalar(out=dst, in0=src, scalar1=fac, scalar2=None, op0=MULT)
+                else:
+                    nc.scalar.activation(out=dst, in_=src, func=COPY, scale=fac)
+            if i + RAW_BUFS < CHUNKS:
+                raws[i + RAW_BUFS] = load_w(i + RAW_BUFS)
+            return grp
+
+        def quant_w(grp):
+            wc = codp.tile([P, HALF], U32, name="wc", align_bytes=64)
+            ws = codp.tile([P, HALF], U8, name="ws", align_bytes=64)
+            nc.vector.quantize_mx(
+                out=wc[:].bitcast(E4M3X4), scales=ws[:], in_=grp[:].rearrange("p w t -> p (w t)")
+            )
+            return wc, ws
+
+        def mx(i, wc, ws, acc):
+            c = i % PASSES
+            for m in range(M_TILES):
+                off = (m * PASSES + c) * P
+                for n in range(2):
+                    nc.tensor.matmul_mx(
+                        out=acc[2 * m + n][:],
+                        lhsT=gc[:, off : off + P].bitcast(E5M2X4),
+                        lhsT_scale=gs[:, off : off + P],
+                        rhs=wc[:, 512 * n : 512 * (n + 1)].bitcast(E4M3X4),
+                        rhs_scale=ws[:, 512 * n : 512 * (n + 1)],
+                        start=(c == 0),
+                        stop=(c == PASSES - 1),
+                    )
+
+        def drain(h, acc):
+            for m in range(M_TILES):
+                ot = outp.tile([P, HALF], F32, name="ot")
+                nc.vector.tensor_copy(out=ot[:, 0:512], in_=acc[2 * m][:])
+                nc.scalar.copy(out=ot[:, 512:1024], in_=acc[2 * m + 1][:])
+                nc.sync.dma_start(
+                    out=o_dram[P * m : P * (m + 1), HALF * h : HALF * (h + 1)], in_=ot[:]
+                )
+
+        def quant_g(m, ggrp, c0, c1):
+            off = (m * PASSES + c0) * P
+            width = (c1 - c0) * P
+            nc.vector.quantize_mx(
+                out=gc[:, off : off + width].bitcast(E5M2X4),
+                scales=gs[:, off : off + width],
+                in_=ggrp[:, K_PASS * c0 : K_PASS * c1],
+            )
+
+        grps = {}
+        codes = {}
+        grps[0] = regroup(0)
+        codes[0] = quant_w(grps[0])
+
+        for m in range(M_TILES):
+            gw = g_sb[m][:].bitcast(F32)
+            ggrp = ggp.tile([P, K_ALL], BF16, name="ggrp", align_bytes=64)
+            gv = ggrp[:].bitcast(F32).rearrange("p (c r u) -> p c r u", r=P, u=2)
+            for j in range(5):
+                ncs = 2 if j < 4 else 1
+                xt = psum.tile([P, 2, 2, P], F32, tag="b%d" % ((5 * m + j) % 8), name="xt")
+                for c2 in range(ncs):
+                    c = 2 * j + c2
+                    for u in range(2):
+                        nc.tensor.transpose(
+                            xt[:, c2, u, :], gw[:, 256 * c + u : 256 * (c + 1) : 2], ident[:]
+                        )
+                src = xt[:, 0:ncs, :, :].rearrange("p c u r -> p c r u")
+                dst = gv[:, 2 * j : 2 * j + ncs, :, :]
+                if j < 3:
+                    nc.scalar.copy(out=dst, in_=src)
+                else:
+                    if j == 3:
+                        quant_g(m, ggrp, 0, 4)
+                    nc.vector.tensor_copy(out=dst, in_=src)
+            quant_g(m, ggrp, 4, 8)
+            quant_g(m, ggrp, 8, 9)
+
+        acc = [psum.tile([P, 512], F32, tag="b%d" % k, name="accA%d" % k) for k in range(8)]
+        mx(0, codes[0][0], codes[0][1], acc)
+        grps[1] = regroup(1)
+        for i in range(1, CHUNKS):
+            if i + 1 < CHUNKS:
+                grps[i + 1] = regroup(i + 1)
+            codes[i] = quant_w(grps[i])
+            if i == PASSES:
+                drain(0, acc)
+                acc = [psum.tile([P, 512], F32, tag="b%d" % k, name="accB%d" % k) for k in range(8)]
+            mx(i, codes[i][0], codes[i][1], acc)
+        drain(1, acc)

@@ -25,6 +25,7 @@ M_TILES = TOKENS // P
 CHUNKS = 2 * PASSES
 RAW_BUFS = 8
 N_VEC = [5, 4, 4]
+TAIL_VEC = [2, 2, 2, 3]
 
 FLOPS = 2 * TOKENS * K_ALL * I_ALL
 BYTES = K_ALL * I_ALL * 2 + TOKENS * K_ALL * 2 + 36 * 16 * 2 + TOKENS * I_ALL * 4
@@ -41,7 +42,7 @@ def tile_gaudifp8linear_kernel(tc, inp, weight, weight_scale_inv, grad_out, out)
         rawp = ctx.enter_context(tc.tile_pool(name="rawp", bufs=RAW_BUFS))
         grpp = ctx.enter_context(tc.tile_pool(name="grpp", bufs=3))
         codp = ctx.enter_context(tc.tile_pool(name="codp", bufs=4))
-        outp = ctx.enter_context(tc.tile_pool(name="outp", bufs=8))
+        outp = ctx.enter_context(tc.tile_pool(name="outp", bufs=4))
         psum = ctx.enter_context(tc.psum_pool(name="psum", bufs=1))
         ctx.enter_context(tc.manual_schedule())
 
@@ -90,56 +91,61 @@ def tile_gaudifp8linear_kernel(tc, inp, weight, weight_scale_inv, grad_out, out)
         gc = const.tile([P, M_TILES * PASSES * P], U32, name="gc", align_bytes=64)
         gs = const.tile([P, M_TILES * PASSES * P], U8, name="gs", align_bytes=64)
 
-        def regroup(i):
+        def regroup(i, blocks, n_vec):
             h, c = divmod(i, PASSES)
             raw = raws[i]
-            n_vec = N_VEC[i % len(N_VEC)]
-            grp = grpp.tile([P, HALF, PACK], BF16, name="grp", align_bytes=64)
-            for b in range(8):
-                cols = slice(P * b, P * (b + 1))
-                dst = grp[:, cols, :].rearrange("p (a i) t -> p a t i", i=4)
-                src = raw[:, :, cols].rearrange("p t (a i) -> p a t i", i=4)
+            grp = grpp.tile([P, P * len(blocks), PACK], BF16, name="grp", tag="grp", align_bytes=64)
+            for k, b in enumerate(blocks):
+                dst = grp[:, P * k : P * (k + 1), :].rearrange("p (a i) t -> p a t i", i=4)
+                src = raw[:, :, P * b : P * (b + 1)].rearrange("p t (a i) -> p a t i", i=4)
                 col = 16 * c + 8 * h + b
                 fac = scl[:, col : col + 1]
-                if b < n_vec:
+                if k < n_vec:
                     nc.vector.tensor_scalar(out=dst, in0=src, scalar1=fac, scalar2=None, op0=MULT)
                 else:
                     nc.scalar.activation(out=dst, in_=src, func=COPY, scale=fac)
-            if i + RAW_BUFS < CHUNKS:
-                raws[i + RAW_BUFS] = load_w(i + RAW_BUFS)
             return grp
 
-        def quant_w(grp):
-            wc = codp.tile([P, HALF], U32, name="wc", align_bytes=64)
-            ws = codp.tile([P, HALF], U8, name="ws", align_bytes=64)
+        def quant_w(grp, width):
+            wc = codp.tile([P, width], U32, name="wc", tag="wc", align_bytes=64)
+            ws = codp.tile([P, width], U8, name="ws", tag="ws", align_bytes=64)
             nc.vector.quantize_mx(
                 out=wc[:].bitcast(E4M3X4), scales=ws[:], in_=grp[:].rearrange("p w t -> p (w t)")
             )
             return wc, ws
 
-        def mx(i, wc, ws, acc):
+        def mx(i, cod, acc, ns):
+            wc, ws = cod
             c = i % PASSES
             for m in range(M_TILES):
                 off = (m * PASSES + c) * P
-                for n in range(2):
+                for k, n in enumerate(ns):
                     nc.tensor.matmul_mx(
                         out=acc[2 * m + n][:],
                         lhsT=gc[:, off : off + P].bitcast(E5M2X4),
                         lhsT_scale=gs[:, off : off + P],
-                        rhs=wc[:, 512 * n : 512 * (n + 1)].bitcast(E4M3X4),
-                        rhs_scale=ws[:, 512 * n : 512 * (n + 1)],
+                        rhs=wc[:, 512 * k : 512 * (k + 1)].bitcast(E4M3X4),
+                        rhs_scale=ws[:, 512 * k : 512 * (k + 1)],
                         start=(c == 0),
                         stop=(c == PASSES - 1),
                     )
 
-        def drain(h, acc):
+        def drain_a(acc):
             for m in range(M_TILES):
-                ot = outp.tile([P, HALF], F32, name="ot")
+                ot = outp.tile([P, HALF], F32, name="ot", tag="ot", bufs=4)
                 nc.vector.tensor_copy(out=ot[:, 0:512], in_=acc[2 * m][:])
                 nc.scalar.copy(out=ot[:, 512:1024], in_=acc[2 * m + 1][:])
-                nc.sync.dma_start(
-                    out=o_dram[P * m : P * (m + 1), HALF * h : HALF * (h + 1)], in_=ot[:]
-                )
+                nc.sync.dma_start(out=o_dram[P * m : P * (m + 1), 0:HALF], in_=ot[:])
+
+        def drain_b(acc, n, engines):
+            for m in range(M_TILES):
+                ob = outp.tile([P, 512], F32, name="ob", tag="ob", bufs=8)
+                if engines[m] == "V":
+                    nc.vector.tensor_copy(out=ob[:], in_=acc[2 * m + n][:])
+                else:
+                    nc.scalar.copy(out=ob[:], in_=acc[2 * m + n][:])
+                lo = HALF + 512 * n
+                nc.sync.dma_start(out=o_dram[P * m : P * (m + 1), lo : lo + 512], in_=ob[:])
 
         def quant_g(m, ggrp, c0, c1):
             off = (m * PASSES + c0) * P
@@ -150,10 +156,12 @@ def tile_gaudifp8linear_kernel(tc, inp, weight, weight_scale_inv, grad_out, out)
                 in_=ggrp[:, K_PASS * c0 : K_PASS * c1],
             )
 
+        all_blocks = list(range(8))
         grps = {}
         codes = {}
-        grps[0] = regroup(0)
-        codes[0] = quant_w(grps[0])
+        grps[0] = regroup(0, all_blocks, N_VEC[0])
+        raws[RAW_BUFS] = load_w(RAW_BUFS)
+        codes[0] = quant_w(grps[0], HALF)
 
         for m in range(M_TILES):
             gw = g_sb[m][:].bitcast(F32)
@@ -180,14 +188,34 @@ def tile_gaudifp8linear_kernel(tc, inp, weight, weight_scale_inv, grad_out, out)
             quant_g(m, ggrp, 8, 9)
 
         acc = [psum.tile([P, 512], F32, tag="b%d" % k, name="accA%d" % k) for k in range(8)]
-        mx(0, codes[0][0], codes[0][1], acc)
-        grps[1] = regroup(1)
-        for i in range(1, CHUNKS):
-            if i + 1 < CHUNKS:
-                grps[i + 1] = regroup(i + 1)
-            codes[i] = quant_w(grps[i])
+        mx(0, codes[0], acc, [0, 1])
+        grps[1] = regroup(1, all_blocks, N_VEC[1])
+        raws[1 + RAW_BUFS] = load_w(1 + RAW_BUFS)
+        whole = CHUNKS - 2
+        tail = [(whole, 0), (whole + 1, 0), (whole, 1), (whole + 1, 1)]
+        tgrp = {}
+
+        def regroup_tail(k):
+            i, n = tail[k]
+            tgrp[k] = regroup(i, all_blocks[4 * n : 4 * n + 4], TAIL_VEC[k])
+
+        for i in range(1, whole):
+            if i + 1 < whole:
+                grps[i + 1] = regroup(i + 1, all_blocks, N_VEC[(i + 1) % len(N_VEC)])
+                if i + 1 + RAW_BUFS < CHUNKS:
+                    raws[i + 1 + RAW_BUFS] = load_w(i + 1 + RAW_BUFS)
+            else:
+                regroup_tail(0)
+            codes[i] = quant_w(grps[i], HALF)
             if i == PASSES:
-                drain(0, acc)
+                drain_a(acc)
                 acc = [psum.tile([P, 512], F32, tag="b%d" % k, name="accB%d" % k) for k in range(8)]
-            mx(i, codes[i][0], codes[i][1], acc)
-        drain(1, acc)
+            mx(i, codes[i], acc, [0, 1])
+        for k in range(4):
+            if k + 1 < 4:
+                regroup_tail(k + 1)
+            cod = quant_w(tgrp[k], 512)
+            if k == 2:
+                drain_b(acc, 0, "SSSS")
+            mx(tail[k][0], cod, acc, [tail[k][1]])
+        drain_b(acc, 1, "SVSV")

@@ -24,7 +24,7 @@ HALF = I_ALL // 2
 M_TILES = TOKENS // P
 CHUNKS = 2 * PASSES
 RAW_BUFS = 8
-N_VEC = [5, 4, 4]
+N_VEC = [4, 4, 4]
 TAIL_VEC = [2, 2, 2, 3]
 
 FLOPS = 2 * TOKENS * K_ALL * I_ALL

@@ -24,8 +24,6 @@ HALF = I_ALL // 2
 M_TILES = TOKENS // P
 CHUNKS = 2 * PASSES
 RAW_BUFS = 8
-N_VEC = [4, 4, 4]
-TAIL_VEC = [2, 2, 2, 3]
 
 FLOPS = 2 * TOKENS * K_ALL * I_ALL
 BYTES = K_ALL * I_ALL * 2 + TOKENS * K_ALL * 2 + 36 * 16 * 2 + TOKENS * I_ALL * 4
@@ -40,8 +38,8 @@ def tile_gaudifp8linear_kernel(tc, inp, weight, weight_scale_inv, grad_out, out)
         const = ctx.enter_context(tc.tile_pool(name="const", bufs=1))
         ggp = ctx.enter_context(tc.tile_pool(name="ggp", bufs=2))
         rawp = ctx.enter_context(tc.tile_pool(name="rawp", bufs=RAW_BUFS))
-        grpp = ctx.enter_context(tc.tile_pool(name="grpp", bufs=3))
-        codp = ctx.enter_context(tc.tile_pool(name="codp", bufs=4))
+        grpp = ctx.enter_context(tc.tile_pool(name="grpp", bufs=6))
+        codp = ctx.enter_context(tc.tile_pool(name="codp", bufs=8))
         outp = ctx.enter_context(tc.tile_pool(name="outp", bufs=4))
         psum = ctx.enter_context(tc.psum_pool(name="psum", bufs=1))
         ctx.enter_context(tc.manual_schedule())
@@ -91,61 +89,78 @@ def tile_gaudifp8linear_kernel(tc, inp, weight, weight_scale_inv, grad_out, out)
         gc = const.tile([P, M_TILES * PASSES * P], U32, name="gc", align_bytes=64)
         gs = const.tile([P, M_TILES * PASSES * P], U8, name="gs", align_bytes=64)
 
-        def regroup(i, blocks, n_vec):
+        units = []
+        for i in range(CHUNKS - 2):
+            units.extend([(i, 0), (i, 1)])
+        units.extend([(CHUNKS - 2, 0), (CHUNKS - 1, 0), (CHUNKS - 2, 1), (CHUNKS - 1, 1)])
+        grps = {}
+        codes = {}
+        acc = {}
+        ots = {}
+
+        def regroup(k):
+            i, n = units[k]
             h, c = divmod(i, PASSES)
+            n_vec = 3 if k == len(units) - 1 else 2
             raw = raws[i]
-            grp = grpp.tile([P, P * len(blocks), PACK], BF16, name="grp", tag="grp", align_bytes=64)
-            for k, b in enumerate(blocks):
-                dst = grp[:, P * k : P * (k + 1), :].rearrange("p (a i) t -> p a t i", i=4)
-                src = raw[:, :, P * b : P * (b + 1)].rearrange("p t (a i) -> p a t i", i=4)
-                col = 16 * c + 8 * h + b
+            grp = grpp.tile([P, 512, PACK], BF16, name="grp", tag="grp", align_bytes=64)
+            for b in range(4):
+                lo = 512 * n + P * b
+                dst = grp[:, P * b : P * (b + 1), :].rearrange("p (a i) t -> p a t i", i=4)
+                src = raw[:, :, lo : lo + P].rearrange("p t (a i) -> p a t i", i=4)
+                col = 16 * c + 8 * h + 4 * n + b
                 fac = scl[:, col : col + 1]
-                if k < n_vec:
+                if b < n_vec:
                     nc.vector.tensor_scalar(out=dst, in0=src, scalar1=fac, scalar2=None, op0=MULT)
                 else:
                     nc.scalar.activation(out=dst, in_=src, func=COPY, scale=fac)
-            return grp
+            grps[k] = grp
+            if n == 1 and i + RAW_BUFS < CHUNKS:
+                raws[i + RAW_BUFS] = load_w(i + RAW_BUFS)
 
-        def quant_w(grp, width):
-            wc = codp.tile([P, width], U32, name="wc", tag="wc", align_bytes=64)
-            ws = codp.tile([P, width], U8, name="ws", tag="ws", align_bytes=64)
+        def quant_w(k):
+            wc = codp.tile([P, 512], U32, name="wc", tag="wc", align_bytes=64)
+            ws = codp.tile([P, 512], U8, name="ws", tag="ws", align_bytes=64)
             nc.vector.quantize_mx(
-                out=wc[:].bitcast(E4M3X4), scales=ws[:], in_=grp[:].rearrange("p w t -> p (w t)")
+                out=wc[:].bitcast(E4M3X4), scales=ws[:], in_=grps[k][:].rearrange("p w t -> p (w t)")
             )
-            return wc, ws
+            codes[k] = (wc, ws)
 
-        def mx(i, cod, acc, ns):
-            wc, ws = cod
+        def mx(k):
+            i, n = units[k]
+            wc, ws = codes[k]
             c = i % PASSES
             for m in range(M_TILES):
                 off = (m * PASSES + c) * P
-                for k, n in enumerate(ns):
-                    nc.tensor.matmul_mx(
-                        out=acc[2 * m + n][:],
-                        lhsT=gc[:, off : off + P].bitcast(E5M2X4),
-                        lhsT_scale=gs[:, off : off + P],
-                        rhs=wc[:, 512 * k : 512 * (k + 1)].bitcast(E4M3X4),
-                        rhs_scale=ws[:, 512 * k : 512 * (k + 1)],
-                        start=(c == 0),
-                        stop=(c == PASSES - 1),
-                    )
+                nc.tensor.matmul_mx(
+                    out=acc[2 * m + n][:],
+                    lhsT=gc[:, off : off + P].bitcast(E5M2X4),
+                    lhsT_scale=gs[:, off : off + P],
+                    rhs=wc[:].bitcast(E4M3X4),
+                    rhs_scale=ws[:],
+                    start=(c == 0),
+                    stop=(c == PASSES - 1),
+                )
 
-        def drain_a(acc):
+        def drain(h, n, engines):
             for m in range(M_TILES):
-                ot = outp.tile([P, HALF], F32, name="ot", tag="ot", bufs=4)
-                nc.vector.tensor_copy(out=ot[:, 0:512], in_=acc[2 * m][:])
-                nc.scalar.copy(out=ot[:, 512:1024], in_=acc[2 * m + 1][:])
-                nc.sync.dma_start(out=o_dram[P * m : P * (m + 1), 0:HALF], in_=ot[:])
-
-        def drain_b(acc, n, engines):
-            for m in range(M_TILES):
-                ob = outp.tile([P, 512], F32, name="ob", tag="ob", bufs=8)
-                if engines[m] == "V":
-                    nc.vector.tensor_copy(out=ob[:], in_=acc[2 * m + n][:])
+                if h == 0:
+                    if n == 0:
+                        ots[m] = outp.tile([P, HALF], F32, name="ot", tag="ot", bufs=4)
+                    dst = ots[m][:, 512 * n : 512 * (n + 1)]
                 else:
-                    nc.scalar.copy(out=ob[:], in_=acc[2 * m + n][:])
-                lo = HALF + 512 * n
-                nc.sync.dma_start(out=o_dram[P * m : P * (m + 1), lo : lo + 512], in_=ob[:])
+                    ob = outp.tile([P, 512], F32, name="ob", tag="ob", bufs=8)
+                    dst = ob[:]
+                if engines[m] == "V":
+                    nc.vector.tensor_copy(out=dst, in_=acc[2 * m + n][:])
+                else:
+                    nc.scalar.copy(out=dst, in_=acc[2 * m + n][:])
+                rows_m = slice(P * m, P * (m + 1))
+                if h == 1:
+                    lo = HALF + 512 * n
+                    nc.sync.dma_start(out=o_dram[rows_m, lo : lo + 512], in_=dst)
+                elif n == 1:
+                    nc.sync.dma_start(out=o_dram[rows_m, 0:HALF], in_=ots[m][:])
 
         def quant_g(m, ggrp, c0, c1):
             off = (m * PASSES + c0) * P
@@ -156,12 +171,10 @@ def tile_gaudifp8linear_kernel(tc, inp, weight, weight_scale_inv, grad_out, out)
                 in_=ggrp[:, K_PASS * c0 : K_PASS * c1],
             )
 
-        all_blocks = list(range(8))
-        grps = {}
-        codes = {}
-        grps[0] = regroup(0, all_blocks, N_VEC[0])
-        raws[RAW_BUFS] = load_w(RAW_BUFS)
-        codes[0] = quant_w(grps[0], HALF)
+        for k in range(2):
+            regroup(k)
+        for k in range(2):
+            quant_w(k)
 
         for m in range(M_TILES):
             gw = g_sb[m][:].bitcast(F32)
@@ -187,35 +200,22 @@ def tile_gaudifp8linear_kernel(tc, inp, weight, weight_scale_inv, grad_out, out)
             quant_g(m, ggrp, 4, 8)
             quant_g(m, ggrp, 8, 9)
 
-        acc = [psum.tile([P, 512], F32, tag="b%d" % k, name="accA%d" % k) for k in range(8)]
-        mx(0, codes[0], acc, [0, 1])
-        grps[1] = regroup(1, all_blocks, N_VEC[1])
-        raws[1 + RAW_BUFS] = load_w(1 + RAW_BUFS)
-        whole = CHUNKS - 2
-        tail = [(whole, 0), (whole + 1, 0), (whole, 1), (whole + 1, 1)]
-        tgrp = {}
-
-        def regroup_tail(k):
-            i, n = tail[k]
-            tgrp[k] = regroup(i, all_blocks[4 * n : 4 * n + 4], TAIL_VEC[k])
-
-        for i in range(1, whole):
-            if i + 1 < whole:
-                grps[i + 1] = regroup(i + 1, all_blocks, N_VEC[(i + 1) % len(N_VEC)])
-                if i + 1 + RAW_BUFS < CHUNKS:
-                    raws[i + 1 + RAW_BUFS] = load_w(i + 1 + RAW_BUFS)
-            else:
-                regroup_tail(0)
-            codes[i] = quant_w(grps[i], HALF)
+        for b in range(8):
+            acc[b] = psum.tile([P, 512], F32, tag="b%d" % b, name="accA%d" % b)
+        for k in range(2):
+            mx(k)
+        regroup(2)
+        for k in range(2, len(units)):
+            i, n = units[k]
+            if k + 1 < len(units):
+                regroup(k + 1)
+            quant_w(k)
             if i == PASSES:
-                drain_a(acc)
-                acc = [psum.tile([P, 512], F32, tag="b%d" % k, name="accB%d" % k) for k in range(8)]
-            mx(i, codes[i], acc, [0, 1])
-        for k in range(4):
-            if k + 1 < 4:
-                regroup_tail(k + 1)
-            cod = quant_w(tgrp[k], 512)
-            if k == 2:
-                drain_b(acc, 0, "SSSS")
-            mx(tail[k][0], cod, acc, [tail[k][1]])
-        drain_b(acc, 1, "SVSV")
+                drain(0, n, "SVSV")
+                for m in range(M_TILES):
+                    b = 2 * m + n
+                    acc[b] = psum.tile([P, 512], F32, tag="b%d" % b, name="accB%d" % b)
+            if k == len(units) - 2:
+                drain(1, 0, "SSSS")
+            mx(k)
+        drain(1, 1, "SVSV")

@@ -24,6 +24,9 @@ HALF = I_ALL // 2
 M_TILES = TOKENS // P
 CHUNKS = 2 * PASSES
 RAW_BUFS = 8
+G_CUT = 4 * K_PASS
+LPAD = 48
+GS_SLOT = 256
 
 FLOPS = 2 * TOKENS * K_ALL * I_ALL
 BYTES = K_ALL * I_ALL * 2 + TOKENS * K_ALL * 2 + 36 * 16 * 2 + TOKENS * I_ALL * 4
@@ -76,7 +79,8 @@ def tile_gaudifp8linear_kernel(tc, inp, weight, weight_scale_inv, grad_out, out)
         g_sb = []
         for m in range(M_TILES):
             g_t = const.tile([P, K_ALL], BF16, name="g%d" % m)
-            nc.sync.dma_start(out=g_t[:], in_=g_dram[P * m : P * (m + 1), :])
+            for lo, hi in ((0, G_CUT), (G_CUT, K_ALL)):
+                nc.sync.dma_start(out=g_t[:, lo:hi], in_=g_dram[P * m : P * (m + 1), lo:hi])
             g_sb.append(g_t)
         for i in range(1, RAW_BUFS):
             raws[i] = load_w(i)
@@ -86,8 +90,8 @@ def tile_gaudifp8linear_kernel(tc, inp, weight, weight_scale_inv, grad_out, out)
         scl = const.tile([P, 16 * PASSES], F32, name="scl")
         nc.vector.tensor_copy(out=scl[:], in_=scl_ps[:, 0 : 16 * PASSES])
 
-        gc = const.tile([P, M_TILES * PASSES * P], U32, name="gc", align_bytes=64)
-        gs = const.tile([P, M_TILES * PASSES * P], U8, name="gs", align_bytes=64)
+        gc = const.tile([P, LPAD + M_TILES * PASSES * P], U32, name="gc", align_bytes=256)
+        gs = const.tile([P, M_TILES * PASSES * GS_SLOT], U8, name="gs", align_bytes=256)
 
         units = []
         for i in range(CHUNKS - 2):
@@ -119,8 +123,8 @@ def tile_gaudifp8linear_kernel(tc, inp, weight, weight_scale_inv, grad_out, out)
                 raws[i + RAW_BUFS] = load_w(i + RAW_BUFS)
 
         def quant_w(k):
-            wc = codp.tile([P, 512], U32, name="wc", tag="wc", align_bytes=64)
-            ws = codp.tile([P, 512], U8, name="ws", tag="ws", align_bytes=64)
+            wc = codp.tile([P, 512], U32, name="wc", tag="wc", align_bytes=256)
+            ws = codp.tile([P, 512], U8, name="ws", tag="ws", align_bytes=256)
             nc.vector.quantize_mx(
                 out=wc[:].bitcast(E4M3X4), scales=ws[:], in_=grps[k][:].rearrange("p w t -> p (w t)")
             )
@@ -131,11 +135,11 @@ def tile_gaudifp8linear_kernel(tc, inp, weight, weight_scale_inv, grad_out, out)
             wc, ws = codes[k]
             c = i % PASSES
             for m in range(M_TILES):
-                off = (m * PASSES + c) * P
+                j = m * PASSES + c
                 nc.tensor.matmul_mx(
                     out=acc[2 * m + n][:],
-                    lhsT=gc[:, off : off + P].bitcast(E5M2X4),
-                    lhsT_scale=gs[:, off : off + P],
+                    lhsT=gc[:, LPAD + P * j : LPAD + P * (j + 1)].bitcast(E5M2X4),
+                    lhsT_scale=gs[:, GS_SLOT * j : GS_SLOT * j + P],
                     rhs=wc[:].bitcast(E4M3X4),
                     rhs_scale=ws[:],
                     start=(c == 0),
@@ -163,13 +167,13 @@ def tile_gaudifp8linear_kernel(tc, inp, weight, weight_scale_inv, grad_out, out)
                     nc.sync.dma_start(out=o_dram[rows_m, 0:HALF], in_=ots[m][:])
 
         def quant_g(m, ggrp, c0, c1):
-            off = (m * PASSES + c0) * P
-            width = (c1 - c0) * P
-            nc.vector.quantize_mx(
-                out=gc[:, off : off + width].bitcast(E5M2X4),
-                scales=gs[:, off : off + width],
-                in_=ggrp[:, K_PASS * c0 : K_PASS * c1],
-            )
+            for c in range(c0, c1):
+                j = m * PASSES + c
+                nc.vector.quantize_mx(
+                    out=gc[:, LPAD + P * j : LPAD + P * (j + 1)].bitcast(E5M2X4),
+                    scales=gs[:, GS_SLOT * j : GS_SLOT * j + P],
+                    in_=ggrp[:, K_PASS * c : K_PASS * (c + 1)],
+                )
 
         for k in range(2):
             regroup(k)

@@ -130,11 +130,11 @@ def tile_gaudifp8linear_kernel(tc, inp, weight, weight_scale_inv, grad_out, out)
             )
             codes[k] = (wc, ws)
 
-        def mx(k):
+        def mx(k, tiles):
             i, n = units[k]
             wc, ws = codes[k]
             c = i % PASSES
-            for m in range(M_TILES):
+            for m in tiles:
                 j = m * PASSES + c
                 nc.tensor.matmul_mx(
                     out=acc[2 * m + n][:],
@@ -206,8 +206,11 @@ def tile_gaudifp8linear_kernel(tc, inp, weight, weight_scale_inv, grad_out, out)
 
         for b in range(8):
             acc[b] = psum.tile([P, 512], F32, tag="b%d" % b, name="accA%d" % b)
+        every = list(range(M_TILES))
+        last = len(units) - 1
+        held = [last - 4, last - 1, last]
         for k in range(2):
-            mx(k)
+            mx(k, every)
         regroup(2)
         for k in range(2, len(units)):
             i, n = units[k]
@@ -221,5 +224,9 @@ def tile_gaudifp8linear_kernel(tc, inp, weight, weight_scale_inv, grad_out, out)
                     acc[b] = psum.tile([P, 512], F32, tag="b%d" % b, name="accB%d" % b)
             if k == len(units) - 2:
                 drain(1, 0, "SSSS")
-            mx(k)
+            if k not in held:
+                mx(k, every)
+        for m in every:
+            for k in held:
+                mx(k, [m])
         drain(1, 1, "SVSV")

@@ -66,12 +66,14 @@ def tile_gaudifp8linear_kernel(tc, inp, weight, weight_scale_inv, grad_out, out)
         def load_w(i):
             h, c = divmod(i, PASSES)
             raw = rawp.tile([P, PACK, HALF], BF16, name="raw")
-            nc.sync.dma_start(
-                out=raw[:],
-                in_=weight[K_PASS * c : K_PASS * (c + 1), HALF * h : HALF * (h + 1)].rearrange(
-                    "(p j) w -> p j w", j=PACK
-                ),
-            )
+            cuts = [0, 512, HALF] if i == CHUNKS - 1 else [0, HALF]
+            for lo, hi in zip(cuts[:-1], cuts[1:]):
+                nc.sync.dma_start(
+                    out=raw[:, :, lo:hi],
+                    in_=weight[K_PASS * c : K_PASS * (c + 1), HALF * h + lo : HALF * h + hi].rearrange(
+                        "(p j) w -> p j w", j=PACK
+                    ),
+                )
             return raw
 
         raws = {}
@@ -130,11 +132,11 @@ def tile_gaudifp8linear_kernel(tc, inp, weight, weight_scale_inv, grad_out, out)
             )
             codes[k] = (wc, ws)
 
-        def mx(k, tiles):
+        def mx(k):
             i, n = units[k]
             wc, ws = codes[k]
             c = i % PASSES
-            for m in tiles:
+            for m in range(M_TILES):
                 j = m * PASSES + c
                 nc.tensor.matmul_mx(
                     out=acc[2 * m + n][:],
@@ -206,11 +208,8 @@ def tile_gaudifp8linear_kernel(tc, inp, weight, weight_scale_inv, grad_out, out)
 
         for b in range(8):
             acc[b] = psum.tile([P, 512], F32, tag="b%d" % b, name="accA%d" % b)
-        every = list(range(M_TILES))
-        last = len(units) - 1
-        held = [last - 4, last - 1, last]
         for k in range(2):
-            mx(k, every)
+            mx(k)
         regroup(2)
         for k in range(2, len(units)):
             i, n = units[k]
@@ -224,9 +223,5 @@ def tile_gaudifp8linear_kernel(tc, inp, weight, weight_scale_inv, grad_out, out)
                     acc[b] = psum.tile([P, 512], F32, tag="b%d" % b, name="accB%d" % b)
             if k == len(units) - 2:
                 drain(1, 0, "SSSS")
-            if k not in held:
-                mx(k, every)
-        for m in every:
-            for k in held:
-                mx(k, [m])
+            mx(k)
         drain(1, 1, "SVSV")

from contextlib import ExitStack

import concourse.mybir as mybir
from concourse.masks import make_identity

F32 = mybir.dt.float32
BF16 = mybir.dt.bfloat16
I32 = mybir.dt.int32
U32 = mybir.dt.uint32
U8 = mybir.dt.uint8
E4M3X4 = mybir.dt.float8_e4m3fn_x4
E5M2X4 = mybir.dt.float8_e5m2_x4
MULT = mybir.AluOpType.mult
COPY = mybir.ActivationFunctionType.Copy

P = 128
PACK = 4
K_PASS = P * PACK
TOKENS = 512
K_ALL = 4608
I_ALL = 2048
PASSES = K_ALL // K_PASS
HALF = I_ALL // 2
M_TILES = TOKENS // P
CHUNKS = 2 * PASSES
RAW_BUFS = 8
G_CUT = 4 * K_PASS
LPAD = 48
GS_SLOT = 256

FLOPS = 2 * TOKENS * K_ALL * I_ALL
BYTES = K_ALL * I_ALL * 2 + TOKENS * K_ALL * 2 + 36 * 16 * 2 + TOKENS * I_ALL * 4


def tile_gaudifp8linear_kernel(tc, inp, weight, weight_scale_inv, grad_out, out):
    nc = tc.nc
    g_dram = grad_out.flatten_outer_dims()
    o_dram = out.flatten_outer_dims()

    with ExitStack() as ctx:
        const = ctx.enter_context(tc.tile_pool(name="const", bufs=1))
        ggp = ctx.enter_context(tc.tile_pool(name="ggp", bufs=2))
        rawp = ctx.enter_context(tc.tile_pool(name="rawp", bufs=RAW_BUFS))
        grpp = ctx.enter_context(tc.tile_pool(name="grpp", bufs=6))
        codp = ctx.enter_context(tc.tile_pool(name="codp", bufs=8))
        outp = ctx.enter_context(tc.tile_pool(name="outp", bufs=4))
        psum = ctx.enter_context(tc.psum_pool(name="psum", bufs=1))
        ctx.enter_context(tc.manual_schedule())

        sel = const.tile([P, P], BF16, name="sel")
        nc.vector.memset(sel[:].bitcast(I32), 0)
        for q in range(4):
            nc.vector.memset(sel[32 * q : 32 * q + 32, 32 * q : 32 * q + 32], 1.0)
        rows = const.tile([P, 256], BF16, name="rows")
        nc.vector.memset(rows[:].bitcast(I32), 0)
        warm = const.tile([P, 2], BF16, name="warm")
        nc.scalar.activation(out=warm[:], in_=sel[:, 0:2], func=COPY)
        ident = const.tile([P, P], F32, name="ident")
        make_identity(nc, ident[:])

        nc.sync.dma_start(
            out=rows[0:P:32, 0 : 16 * PASSES].rearrange("q (c n) -> q c n", n=16),
            in_=weight_scale_inv.rearrange("(c q) n -> q c n", q=4),
        )

        def load_w(i):
            h, c = divmod(i, PASSES)
            raw = rawp.tile([P, PACK, HALF], BF16, name="raw")
            cuts = [0, 512, HALF] if i == CHUNKS - 1 else [0, HALF]
            for lo, hi in zip(cuts[:-1], cuts[1:]):
                nc.sync.dma_start(
                    out=raw[:, :, lo:hi],
                    in_=weight[K_PASS * c : K_PASS * (c + 1), HALF * h + lo : HALF * h + hi].rearrange(
                        "(p j) w -> p j w", j=PACK
                    ),
                )
            return raw

        raws = {}
        raws[0] = load_w(0)
        g_sb = []
        for m in range(M_TILES):
            g_t = const.tile([P, K_ALL], BF16, name="g%d" % m)
            for lo, hi in ((0, G_CUT), (G_CUT, K_ALL)):
                nc.sync.dma_start(out=g_t[:, lo:hi], in_=g_dram[P * m : P * (m + 1), lo:hi])
            g_sb.append(g_t)
        for i in range(1, RAW_BUFS):
            raws[i] = load_w(i)

        scl_ps = psum.tile([P, 512], F32, tag="b7", name="scl_ps")
        nc.tensor.matmul(scl_ps[:, 0:256], lhsT=sel[:], rhs=rows[:], start=True, stop=True)
        scl = const.tile([P, 16 * PASSES], F32, name="scl")
        nc.vector.tensor_copy(out=scl[:], in_=scl_ps[:, 0 : 16 * PASSES])

        gc = const.tile([P, LPAD + M_TILES * PASSES * P], U32, name="gc", align_bytes=256)
        gs = const.tile([P, M_TILES * PASSES * GS_SLOT], U8, name="gs", align_bytes=256)

        units = []
        for i in range(CHUNKS - 2):
            units.extend([(i, 0), (i, 1)])
        units.extend([(CHUNKS - 2, 0), (CHUNKS - 1, 0), (CHUNKS - 2, 1), (CHUNKS - 1, 1)])
        grps = {}
        codes = {}
        acc = {}
        ots = {}

        def regroup(k):
            i, n = units[k]
            h, c = divmod(i, PASSES)
            n_vec = 3 if k == len(units) - 1 else 2
            raw = raws[i]
            grp = grpp.tile([P, 512, PACK], BF16, name="grp", tag="grp", align_bytes=64)
            for b in range(4):
                lo = 512 * n + P * b
                dst = grp[:, P * b : P * (b + 1), :].rearrange("p (a i) t -> p a t i", i=4)
                src = raw[:, :, lo : lo + P].rearrange("p t (a i) -> p a t i", i=4)
                col = 16 * c + 8 * h + 4 * n + b
                fac = scl[:, col : col + 1]
                if b < n_vec:
                    nc.vector.tensor_scalar(out=dst, in0=src, scalar1=fac, scalar2=None, op0=MULT)
                else:
                    nc.scalar.activation(out=dst, in_=src, func=COPY, scale=fac)
            grps[k] = grp
            if n == 1 and i + RAW_BUFS < CHUNKS:
                raws[i + RAW_BUFS] = load_w(i + RAW_BUFS)

        def quant_w(k):
            wc = codp.tile([P, 512], U32, name="wc", tag="wc", align_bytes=256)
            ws = codp.tile([P, 512], U8, name="ws", tag="ws", align_bytes=256)
            nc.vector.quantize_mx(
                out=wc[:].bitcast(E4M3X4), scales=ws[:], in_=grps[k][:].rearrange("p w t -> p (w t)")
            )
            codes[k] = (wc, ws)

        def mx(k):
            i, n = units[k]
            wc, ws = codes[k]
            c = i % PASSES
            for m in range(M_TILES):
                j = m * PASSES + c
                nc.tensor.matmul_mx(
                    out=acc[2 * m + n][:],
                    lhsT=gc[:, LPAD + P * j : LPAD + P * (j + 1)].bitcast(E5M2X4),
                    lhsT_scale=gs[:, GS_SLOT * j : GS_SLOT * j + P],
                    rhs=wc[:].bitcast(E4M3X4),
                    rhs_scale=ws[:],
                    start=(c == 0),
                    stop=(c == PASSES - 1),
                )

        def drain(h, n, engines):
            for m in range(M_TILES):
                if h == 0:
                    if n == 0:
                        ots[m] = outp.tile([P, HALF], F32, name="ot", tag="ot", bufs=4)
                    dst = ots[m][:, 512 * n : 512 * (n + 1)]
                else:
                    ob = outp.tile([P, 512], F32, name="ob", tag="ob", bufs=8)
                    dst = ob[:]
                if engines[m] == "V":
                    nc.vector.tensor_copy(out=dst, in_=acc[2 * m + n][:])
                else:
                    nc.scalar.copy(out=dst, in_=acc[2 * m + n][:])
                rows_m = slice(P * m, P * (m + 1))
                if h == 1:
                    lo = HALF + 512 * n
                    nc.sync.dma_start(out=o_dram[rows_m, lo : lo + 512], in_=dst)
                elif n == 1:
                    nc.sync.dma_start(out=o_dram[rows_m, 0:HALF], in_=ots[m][:])

        def quant_g(m, ggrp, c0, c1):
            for c in range(c0, c1):
                j = m * PASSES + c
                nc.vector.quantize_mx(
                    out=gc[:, LPAD + P * j : LPAD + P * (j + 1)].bitcast(E5M2X4),
                    scales=gs[:, GS_SLOT * j : GS_SLOT * j + P],
                    in_=ggrp[:, K_PASS * c : K_PASS * (c + 1)],
                )

        for k in range(2):
            regroup(k)
        for k in range(2):
            quant_w(k)

        for m in range(M_TILES):
            gw = g_sb[m][:].bitcast(F32)
            ggrp = ggp.tile([P, K_ALL], BF16, name="ggrp", align_bytes=64)
            gv = ggrp[:].bitcast(F32).rearrange("p (c r u) -> p c r u", r=P, u=2)
            for j in range(5):
                ncs = 2 if j < 4 else 1
                xt = psum.tile([P, 2, 2, P], F32, tag="b%d" % ((5 * m + j) % 8), name="xt")
                for c2 in range(ncs):
                    c = 2 * j + c2
                    for u in range(2):
                        nc.tensor.transpose(
                            xt[:, c2, u, :], gw[:, 256 * c + u : 256 * (c + 1) : 2], ident[:]
                        )
                src = xt[:, 0:ncs, :, :].rearrange("p c u r -> p c r u")
                dst = gv[:, 2 * j : 2 * j + ncs, :, :]
                if j < 3:
                    nc.scalar.copy(out=dst, in_=src)
                else:
                    if j == 3:
                        quant_g(m, ggrp, 0, 4)
                    nc.vector.tensor_copy(out=dst, in_=src)
            quant_g(m, ggrp, 4, 8)
            quant_g(m, ggrp, 8, 9)

        for b in range(8):
            acc[b] = psum.tile([P, 512], F32, tag="b%d" % b, name="accA%d" % b)
        for k in range(2):
            mx(k)
        regroup(2)
        for k in range(2, len(units)):
            i, n = units[k]
            if k + 1 < len(units):
                regroup(k + 1)
            quant_w(k)
            if i == PASSES:
                drain(0, n, "SVSV")
                for m in range(M_TILES):
                    b = 2 * m + n
                    acc[b] = psum.tile([P, 512], F32, tag="b%d" % b, name="accB%d" % b)
            if k == len(units) - 2:
                drain(1, 0, "SSSS")
            mx(k)
        drain(1, 1, "SVSV")
